import numpy as np
import ml_dtypes


def mxq(x, axis, fmt="e4m3"):
    dtype, down = {"e4m3": (ml_dtypes.float8_e4m3fn, 7), "e5m2": (ml_dtypes.float8_e5m2, 14)}[fmt]
    v = np.moveaxis(np.asarray(x, np.float32).astype(ml_dtypes.bfloat16).astype(np.float64), axis, -1)
    blocks = v.reshape(v.shape[:-1] + (-1, 32))
    amax = np.abs(blocks).max(-1, keepdims=True)
    byte = np.maximum(np.where(amax > 0, np.frexp(amax)[1] - 1 + 127, 0) - down, 1)
    scale = np.exp2(byte - 127.0)
    codes = (blocks / scale).astype(np.float32).astype(dtype).astype(np.float64)
    return np.moveaxis((codes * scale).reshape(v.shape), -1, axis)


WIDE = False


def mx_kscale(k):
    if not WIDE:
        return np.ones(k)
    levels = np.array([10, -10, 5, -5, 0])
    a = np.random.permutation(np.resize(levels, k // 512 * 4)).reshape(k // 512, 4)
    idx = np.arange(k)
    return np.exp2(a[idx // 512, idx % 128 // 32])


BF16 = ml_dtypes.bfloat16


def bf(x):
    return np.asarray(x, np.float32).astype(BF16)


def f64(x):
    return np.asarray(x).astype(np.float64)


B, L, E, H, HD, F, G = 4, 128, 1024, 8, 128, 2048, 2048
EPS = 1e-6


def rmsnorm(x, g):
    return x * (1.0 / np.sqrt(np.mean(x * x, axis=-1, keepdims=True) + EPS)) * g


def rope_diag():
    pair = np.arange(HD) // 2
    theta = 10000.0 ** (-2.0 * pair / HD)
    return np.cos(np.arange(L)[:, None] * theta[None, :])


def setup_inputs():
    s = mx_kscale(E)
    return {"x": bf(np.random.standard_normal((B, L, E))),
            "g": bf((1.0 + 0.1 * np.random.standard_normal(E)) * s),
            "wq": bf(np.random.standard_normal((E, H * HD)) / np.sqrt(E) / s[:, None]),
            "wk": bf(np.random.standard_normal((E, H * HD)) / np.sqrt(E) / s[:, None])}


def reference(x, g, wq, wk):
    hq = mxq(rmsnorm(f64(x), f64(g)), 2, "e4m3")
    c = rope_diag()
    q = (hq @ mxq(f64(wq), 0, "e4m3")).reshape(B, L, H, HD).transpose(0, 2, 1, 3) * c
    k = (hq @ mxq(f64(wk), 0, "e4m3")).reshape(B, L, H, HD).transpose(0, 2, 1, 3) * c
    return q, k

@@ -1,0 +1,203 @@
+import math
+from contextlib import ExitStack
+
+import concourse.mybir as mybir
+
+FP8X4 = mybir.dt.float8_e4m3fn_x4
+BF16 = mybir.dt.bfloat16
+F32 = mybir.dt.float32
+I32 = mybir.dt.int32
+U32 = mybir.dt.uint32
+U8 = mybir.dt.uint8
+ALU = mybir.AluOpType
+ACT = mybir.ActivationFunctionType
+
+P = 128
+B, L, E, H, HD = 4, 128, 1024, 8, 128
+EPS = 1e-6
+FLOPS = 2 * B * L * E * 2 * H * HD
+NT = 4
+NCH = 4
+NG = 2
+VCOLS = [448, 288, 160, 0, 160, 224, 0, 0]
+TURN = 1.0 / (2.0 * math.pi)
+
+
+def tile_llamaselfattentionblock_pa_kernel(tc, x, g, wq, wk, out_0, out_1):
+    nc = tc.nc
+    with ExitStack() as ctx:
+        const = ctx.enter_context(tc.tile_pool(name="const", bufs=1))
+        work = ctx.enter_context(tc.tile_pool(name="work", bufs=2))
+        gpool = ctx.enter_context(tc.tile_pool(name="gpool", bufs=3))
+        opool = ctx.enter_context(tc.tile_pool(name="opool", bufs=3))
+        psum = ctx.enter_context(tc.psum_pool(name="psum", bufs=8))
+
+        grow = const.tile([P, E], BF16)
+        nc.vector.memset(grow[:], 0.0)
+        nc.sync.dma_start(out=grow[0:1, :], in_=g.rearrange("(o k) -> o k", o=1))
+        xv = x.rearrange("b l k -> (b l) k").rearrange("(p j) k -> p j k", j=NT)
+        xt = []
+        for j in range(NT):
+            xj = const.tile([P, E], BF16, name="x%d" % j)
+            nc.sync.dma_start(out=xj[:], in_=xv[:, j, :])
+            xt.append(xj)
+        wr = []
+        for c in range(NCH):
+            w = wq if c < 2 else wk
+            n0 = 512 * (c % 2)
+            for gg in range(NG):
+                wt = const.tile([P, 4, 512], BF16, name="wr%d" % (c * NG + gg))
+                nc.sync.dma_start(
+                    out=wt[:],
+                    in_=w[512 * gg : 512 * gg + 512, n0 : n0 + 512].rearrange("(t p) n -> p t n", p=P),
+                )
+                wr.append(wt)
+
+        ones = const.tile([P, P], BF16)
+        nc.vector.memset(ones[:], 1.0)
+        neghalf = const.tile([P, 1], F32)
+        nc.vector.memset(neghalf[:], -0.5)
+        pidx = const.tile([P, 1], I32)
+        nc.gpsimd.iota(pidx[:], pattern=[[0, 1]], base=0, channel_multiplier=1)
+        colsi = const.tile([P, P], I32)
+        nc.gpsimd.iota(colsi[:], pattern=[[1, P]], base=0, channel_multiplier=0)
+
+        th = const.tile([P, 64], F32)
+        nc.vector.memset(th[:, 0:1], 1.0)
+        ratio = 10000.0 ** (-1.0 / 64.0)
+        for s in range(6):
+            wd = 1 << s
+            nc.vector.tensor_scalar(
+                out=th[:, wd : 2 * wd], in0=th[:, 0:wd], scalar1=ratio**wd, scalar2=None, op0=ALU.mult
+            )
+        jt = const.tile([P, NT, 64], F32)
+        for j in range(NT):
+            nc.vector.tensor_scalar(
+                out=jt[:, j, :], in0=th[:], scalar1=j * TURN, scalar2=0.25, op0=ALU.mult, op1=ALU.add
+            )
+        pa = const.tile([P, 1], I32)
+        nc.vector.tensor_scalar(
+            out=pa[:], in0=pidx[:], scalar1=31, scalar2=2, op0=ALU.bitwise_and, op1=ALU.logical_shift_left
+        )
+        pb = const.tile([P, 1], I32)
+        nc.vector.tensor_scalar(out=pb[:], in0=pidx[:], scalar1=5, scalar2=None, op0=ALU.logical_shift_right)
+        pm = const.tile([P, 1], I32)
+        nc.vector.tensor_tensor(out=pm[:], in0=pa[:], in1=pb[:], op=ALU.bitwise_or)
+        pmf = const.tile([P, 1], F32)
+        nc.vector.tensor_copy(out=pmf[:], in_=pm[:])
+        colsf = const.tile([P, P], F32)
+        nc.vector.tensor_copy(out=colsf[:], in_=colsi[:])
+        perm = const.tile([P, P], BF16)
+        nc.vector.tensor_scalar(out=perm[:], in0=colsf[:], scalar1=pmf[:, 0:1], scalar2=None, op0=ALU.is_equal)
+        l0i = const.tile([P, 1], I32)
+        nc.vector.tensor_scalar(out=l0i[:], in0=pidx[:], scalar1=124, scalar2=None, op0=ALU.bitwise_and)
+        l0f = const.tile([P, 1], F32)
+        nc.vector.tensor_scalar(out=l0f[:], in0=l0i[:], scalar1=TURN, scalar2=None, op0=ALU.mult)
+        yy = const.tile([P, NT, 64], F32)
+        nc.vector.scalar_tensor_tensor(
+            out=yy[:],
+            in0=th[:].unsqueeze(1).to_broadcast([P, NT, 64]),
+            scalar=l0f[:, 0:1],
+            in1=jt[:],
+            op0=ALU.mult,
+            op1=ALU.add,
+        )
+        yi = const.tile([P, NT, 64], I32)
+        nc.vector.tensor_copy(out=yi[:], in_=yy[:])
+        yf = const.tile([P, NT, 64], F32)
+        nc.vector.tensor_copy(out=yf[:], in_=yi[:])
+        rr = const.tile([P, NT, 64], F32)
+        nc.vector.tensor_tensor(out=rr[:], in0=yy[:], in1=yf[:], op=ALU.subtract)
+        nr = const.tile([P, NT, 64], F32)
+        nc.vector.scalar_tensor_tensor(
+            out=nr[:], in0=rr[:], scalar=0.5, in1=rr[:], op0=ALU.is_gt, op1=ALU.subtract
+        )
+        ctab = const.tile([P, NT, 64, 2], F32)
+        nc.scalar.activation(
+            out=ctab[:],
+            in_=nr[:].unsqueeze(3).to_broadcast([P, NT, 64, 2]),
+            func=ACT.Sin,
+            scale=-2.0 * math.pi,
+        )
+
+        gps = []
+        for hf in range(2):
+            gp = psum.tile([P, 512], F32, tag="bank", name="gp%d" % hf)
+            nc.tensor.matmul(out=gp[:], lhsT=ones[:], rhs=grow[:, 512 * hf : 512 * hf + 512], start=True, stop=True)
+            gps.append(gp)
+
+        hw = const.tile([P, NT, 256], U32, align_bytes=64)
+        hs = const.tile([P, NT, 256], U8, align_bytes=64)
+        for j in range(NT):
+            junk = work.tile([P, E], BF16, tag="junk")
+            ms = const.tile([P, 1], F32, name="ms%d" % j)
+            nc.scalar.activation(out=junk[:], in_=xt[j][:], func=ACT.Square, scale=1.0 / 32.0, accum_out=ms[:])
+            me = const.tile([P, 1], F32, name="me%d" % j)
+            nc.gpsimd.tensor_scalar(out=me[:], in0=ms[:], scalar1=1.0, scalar2=EPS, op0=ALU.mult, op1=ALU.add)
+            rstd = const.tile([P, 1], F32, name="rstd%d" % j)
+            nc.gpsimd.tensor_tensor(out=rstd[:], in0=me[:], in1=neghalf[:], op=ALU.pow)
+            hj = const.tile([P, E], BF16, name="h%d" % j)
+            for hf in range(2):
+                sl = slice(512 * hf, 512 * hf + 512)
+                nc.vector.scalar_tensor_tensor(
+                    out=hj[:, sl], in0=xt[j][:, sl], scalar=rstd[:, 0:1], in1=gps[hf][:], op0=ALU.mult, op1=ALU.mult
+                )
+            tp = psum.tile([P, 8, P], BF16, tag="bank", name="tp%d" % j)
+            for q in range(8):
+                nc.tensor.transpose(out=tp[:, q, :], in_=hj[:, P * q : P * q + P], identity=perm[:])
+            hg = const.tile([P, NG, P, 4], BF16, name="hg%d" % j, align_bytes=64)
+            nc.scalar.copy(out=hg[:], in_=tp[:].rearrange("p (g t) l -> p g l t", t=4))
+            nc.vector.quantize_mx(
+                out=hw[:, j, :].bitcast(FP8X4),
+                scales=hs[:, j, :],
+                in_=hg[:].rearrange("p g l t -> p (g l t)"),
+            )
+
+        for c in range(NCH):
+            om = out_0 if c < 2 else out_1
+            h0 = 4 * (c % 2)
+            wws = []
+            for gg in range(NG):
+                u = c * NG + gg
+                wg = gpool.tile([P, 512, 4], BF16, tag="wg", align_bytes=64)
+                vc = VCOLS[u]
+                if vc > 0:
+                    nc.vector.tensor_copy(
+                        out=wg[:, 0:vc, :].rearrange("p (c i) t -> p c t i", i=4),
+                        in_=wr[u][:, :, 0:vc].rearrange("p t (c i) -> p c t i", i=4),
+                    )
+                if vc < 512:
+                    nc.scalar.copy(
+                        out=wg[:, vc:512, :].rearrange("p (c i) t -> p c t i", i=4),
+                        in_=wr[u][:, :, vc:512].rearrange("p t (c i) -> p c t i", i=4),
+                    )
+                ww = const.tile([P, 512], U32, name="ww%d" % u, align_bytes=64)
+                ws = const.tile([P, 512], U8, name="ws%d" % u, align_bytes=64)
+                nc.vector.quantize_mx(
+                    out=ww[:].bitcast(FP8X4), scales=ws[:], in_=wg[:].rearrange("p n t -> p (n t)")
+                )
+                wws.append((ww, ws))
+            osb = opool.tile([P, 4, NT, HD], F32, tag="osb")
+            for j in range(NT):
+                acc = psum.tile([P, 512], F32, tag="bank", name="acc")
+                for gg in range(NG):
+                    nc.tensor.matmul_mx(
+                        out=acc[:],
+                        lhsT=hw[:, j, P * gg : P * gg + P].bitcast(FP8X4),
+                        lhsT_scale=hs[:, j, P * gg : P * gg + P],
+                        rhs=wws[gg][0][:].bitcast(FP8X4),
+                        rhs_scale=wws[gg][1][:],
+                        start=(gg == 0),
+                        stop=(gg == NG - 1),
+                    )
+                nc.vector.tensor_tensor(
+                    out=osb[:, :, j, :],
+                    in0=acc[:].rearrange("p (n d) -> p n d", d=HD),
+                    in1=ctab[:, j, :, :].rearrange("p i e -> p (i e)").unsqueeze(1).to_broadcast([P, 4, HD]),
+                    op=ALU.mult,
+                )
+            for b in range(B):
+                nc.sync.dma_start(
+                    out=om[b, h0 : h0 + 4, :, :].rearrange("n (lh j) d -> lh n (j d)", j=NT),
+                    in_=osb[b:P:4, :, :, :].rearrange("p n j d -> p n (j d)"),
+                )

@@ -17,39 +17,44 @@ B, L, E, H, HD = 4, 128, 1024, 8, 128
 EPS = 1e-6
 FLOPS = 2 * B * L * E * 2 * H * HD
 NT = 4
-NCH = 4
 NG = 2
-VCOLS = [448, 288, 160, 0, 160, 224, 0, 0]
 TURN = 1.0 / (2.0 * math.pi)
+CHUNKS = [(0, 0, 512), (0, 512, 512), (1, 0, 512), (1, 512, 256), (1, 768, 256)]
+VCOLS = [288, 320, 192, 160, 0, 0, 0, 96, 0, 0]
+SPLIT_STATS = [True, True, False, False]
+S_PRE = 2
+HQ_POS = [2, 3, 4, 4]
+PIN = True
 
 
 def tile_llamaselfattentionblock_pa_kernel(tc, x, g, wq, wk, out_0, out_1):
     nc = tc.nc
+    nu = NG * len(CHUNKS)
     with ExitStack() as ctx:
         const = ctx.enter_context(tc.tile_pool(name="const", bufs=1))
-        work = ctx.enter_context(tc.tile_pool(name="work", bufs=2))
-        gpool = ctx.enter_context(tc.tile_pool(name="gpool", bufs=3))
-        opool = ctx.enter_context(tc.tile_pool(name="opool", bufs=3))
         psum = ctx.enter_context(tc.psum_pool(name="psum", bufs=8))
+        if PIN:
+            ctx.enter_context(tc.manual_schedule())
 
         grow = const.tile([P, E], BF16)
         nc.vector.memset(grow[:], 0.0)
-        nc.sync.dma_start(out=grow[0:1, :], in_=g.rearrange("(o k) -> o k", o=1))
         xv = x.rearrange("b l k -> (b l) k").rearrange("(p j) k -> p j k", j=NT)
         xt = []
         for j in range(NT):
             xj = const.tile([P, E], BF16, name="x%d" % j)
             nc.sync.dma_start(out=xj[:], in_=xv[:, j, :])
             xt.append(xj)
+            if j == 0:
+                nc.sync.dma_start(out=grow[0:1, :], in_=g.rearrange("(o k) -> o k", o=1))
         wr = []
-        for c in range(NCH):
-            w = wq if c < 2 else wk
-            n0 = 512 * (c % 2)
+        for c in range(len(CHUNKS)):
+            m, n0, wd = CHUNKS[c]
+            w = wq if m == 0 else wk
             for gg in range(NG):
-                wt = const.tile([P, 4, 512], BF16, name="wr%d" % (c * NG + gg))
+                wt = const.tile([P, 4, wd], BF16, name="wr%d" % (c * NG + gg))
                 nc.sync.dma_start(
                     out=wt[:],
-                    in_=w[512 * gg : 512 * gg + 512, n0 : n0 + 512].rearrange("(t p) n -> p t n", p=P),
+                    in_=w[512 * gg : 512 * gg + 512, n0 : n0 + wd].rearrange("(t p) n -> p t n", p=P),
                 )
                 wr.append(wt)
 
@@ -57,6 +62,8 @@ def tile_llamaselfattentionblock_pa_kernel(tc, x, g, wq, wk, out_0, out_1):
         nc.vector.memset(ones[:], 1.0)
         neghalf = const.tile([P, 1], F32)
         nc.vector.memset(neghalf[:], -0.5)
+        warm = const.tile([P, 1], F32)
+        nc.scalar.activation(out=warm[:], in_=neghalf[:], func=ACT.Sin)
         pidx = const.tile([P, 1], I32)
         nc.gpsimd.iota(pidx[:], pattern=[[0, 1]], base=0, channel_multiplier=1)
         colsi = const.tile([P, P], I32)
@@ -93,6 +100,13 @@ def tile_llamaselfattentionblock_pa_kernel(tc, x, g, wq, wk, out_0, out_1):
         nc.vector.tensor_scalar(out=l0i[:], in0=pidx[:], scalar1=124, scalar2=None, op0=ALU.bitwise_and)
         l0f = const.tile([P, 1], F32)
         nc.vector.tensor_scalar(out=l0f[:], in0=l0i[:], scalar1=TURN, scalar2=None, op0=ALU.mult)
+
+        gps = []
+        for hf in range(2):
+            gp = psum.tile([P, 512], F32, tag="bank", name="gp%d" % hf)
+            nc.tensor.matmul(out=gp[:], lhsT=ones[:], rhs=grow[:, 512 * hf : 512 * hf + 512], start=True, stop=True)
+            gps.append(gp)
+
         yy = const.tile([P, NT, 64], F32)
         nc.vector.scalar_tensor_tensor(
             out=yy[:],
@@ -112,6 +126,37 @@ def tile_llamaselfattentionblock_pa_kernel(tc, x, g, wq, wk, out_0, out_1):
         nc.vector.scalar_tensor_tensor(
             out=nr[:], in0=rr[:], scalar=0.5, in1=rr[:], op0=ALU.is_gt, op1=ALU.subtract
         )
+        rstds = []
+        for j in range(NT):
+            me = const.tile([P, 1], F32, name="me%d" % j)
+            msa = const.tile([P, 1], F32, name="msa%d" % j)
+            if SPLIT_STATS[j]:
+                junka = const.tile([P, 512], BF16, name="junka%d" % j)
+                nc.scalar.activation(
+                    out=junka[:], in_=xt[j][:, 0:512], func=ACT.Square, scale=1.0 / 32.0, accum_out=msa[:]
+                )
+                junkb = const.tile([P, 512], F32, name="junkb%d" % j)
+                msb = const.tile([P, 1], F32, name="msb%d" % j)
+                nc.vector.scalar_tensor_tensor(
+                    out=junkb[:],
+                    in0=xt[j][:, 512:1024],
+                    scalar=1.0 / 1024.0,
+                    in1=xt[j][:, 512:1024],
+                    op0=ALU.mult,
+                    op1=ALU.mult,
+                    accum_out=msb[:],
+                )
+                nc.gpsimd.tensor_scalar(
+                    out=me[:], in0=msa[:], scalar1=msb[:, 0:1], scalar2=EPS, op0=ALU.add, op1=ALU.add
+                )
+            else:
+                junka = const.tile([P, E], BF16, name="junka%d" % j)
+                nc.scalar.activation(out=junka[:], in_=xt[j][:], func=ACT.Square, scale=1.0 / 32.0, accum_out=msa[:])
+                nc.gpsimd.tensor_scalar(out=me[:], in0=msa[:], scalar1=1.0, scalar2=EPS, op0=ALU.mult, op1=ALU.add)
+            rstd = const.tile([P, 1], F32, name="rstd%d" % j)
+            nc.gpsimd.tensor_tensor(out=rstd[:], in0=me[:], in1=neghalf[:], op=ALU.pow)
+            rstds.append(rstd)
+
         ctab = const.tile([P, NT, 64, 2], F32)
         nc.scalar.activation(
             out=ctab[:],
@@ -120,84 +165,136 @@ def tile_llamaselfattentionblock_pa_kernel(tc, x, g, wq, wk, out_0, out_1):
             scale=-2.0 * math.pi,
         )
 
-        gps = []
-        for hf in range(2):
-            gp = psum.tile([P, 512], F32, tag="bank", name="gp%d" % hf)
-            nc.tensor.matmul(out=gp[:], lhsT=ones[:], rhs=grow[:, 512 * hf : 512 * hf + 512], start=True, stop=True)
-            gps.append(gp)
-
-        hw = const.tile([P, NT, 256], U32, align_bytes=64)
-        hs = const.tile([P, NT, 256], U8, align_bytes=64)
+        tps = []
         for j in range(NT):
-            junk = work.tile([P, E], BF16, tag="junk")
-            ms = const.tile([P, 1], F32, name="ms%d" % j)
-            nc.scalar.activation(out=junk[:], in_=xt[j][:], func=ACT.Square, scale=1.0 / 32.0, accum_out=ms[:])
-            me = const.tile([P, 1], F32, name="me%d" % j)
-            nc.gpsimd.tensor_scalar(out=me[:], in0=ms[:], scalar1=1.0, scalar2=EPS, op0=ALU.mult, op1=ALU.add)
-            rstd = const.tile([P, 1], F32, name="rstd%d" % j)
-            nc.gpsimd.tensor_tensor(out=rstd[:], in0=me[:], in1=neghalf[:], op=ALU.pow)
             hj = const.tile([P, E], BF16, name="h%d" % j)
             for hf in range(2):
                 sl = slice(512 * hf, 512 * hf + 512)
                 nc.vector.scalar_tensor_tensor(
-                    out=hj[:, sl], in0=xt[j][:, sl], scalar=rstd[:, 0:1], in1=gps[hf][:], op0=ALU.mult, op1=ALU.mult
+                    out=hj[:, sl],
+                    in0=xt[j][:, sl],
+                    scalar=rstds[j][:, 0:1],
+                    in1=gps[hf][:],
+                    op0=ALU.mult,
+                    op1=ALU.mult,
                 )
             tp = psum.tile([P, 8, P], BF16, tag="bank", name="tp%d" % j)
             for q in range(8):
                 nc.tensor.transpose(out=tp[:, q, :], in_=hj[:, P * q : P * q + P], identity=perm[:])
+            tps.append(tp)
+
+        wgs = []
+        for u in range(nu):
+            wd = CHUNKS[u // NG][2]
+            wgs.append(const.tile([P, wd, 4], BF16, name="wg%d" % u, align_bytes=64))
+
+        def regroup(eng_copy, u, c0, c1):
+            eng_copy(
+                out=wgs[u][:, c0:c1, :].rearrange("p (c i) t -> p c t i", i=4),
+                in_=wr[u][:, :, c0:c1].rearrange("p t (c i) -> p c t i", i=4),
+            )
+
+        def regroup_s(u):
+            wd = CHUNKS[u // NG][2]
+            if VCOLS[u] < wd:
+                regroup(nc.scalar.copy, u, VCOLS[u], wd)
+
+        def regroup_v(u):
+            if VCOLS[u] > 0:
+                regroup(nc.vector.tensor_copy, u, 0, VCOLS[u])
+
+        for u in range(S_PRE):
+            regroup_s(u)
+        hgs = []
+        for j in range(NT):
             hg = const.tile([P, NG, P, 4], BF16, name="hg%d" % j, align_bytes=64)
-            nc.scalar.copy(out=hg[:], in_=tp[:].rearrange("p (g t) l -> p g l t", t=4))
+            nc.scalar.copy(out=hg[:], in_=tps[j][:].rearrange("p (g t) l -> p g l t", t=4))
+            hgs.append(hg)
+        for u in range(S_PRE, nu):
+            regroup_s(u)
+
+        hw = const.tile([P, NT, 256], U32, align_bytes=64)
+        hs = const.tile([P, NT, 256], U8, align_bytes=64)
+        wws = []
+        accs = []
+        state = {"hq": 0, "passes": 0}
+
+        def h_quant(j):
             nc.vector.quantize_mx(
                 out=hw[:, j, :].bitcast(FP8X4),
                 scales=hs[:, j, :],
-                in_=hg[:].rearrange("p g l t -> p (g l t)"),
+                in_=hgs[j][:].rearrange("p g l t -> p (g l t)"),
             )
 
-        for c in range(NCH):
-            om = out_0 if c < 2 else out_1
-            h0 = 4 * (c % 2)
-            wws = []
-            for gg in range(NG):
-                u = c * NG + gg
-                wg = gpool.tile([P, 512, 4], BF16, tag="wg", align_bytes=64)
-                vc = VCOLS[u]
-                if vc > 0:
-                    nc.vector.tensor_copy(
-                        out=wg[:, 0:vc, :].rearrange("p (c i) t -> p c t i", i=4),
-                        in_=wr[u][:, :, 0:vc].rearrange("p t (c i) -> p c t i", i=4),
-                    )
-                if vc < 512:
-                    nc.scalar.copy(
-                        out=wg[:, vc:512, :].rearrange("p (c i) t -> p c t i", i=4),
-                        in_=wr[u][:, :, vc:512].rearrange("p t (c i) -> p c t i", i=4),
-                    )
-                ww = const.tile([P, 512], U32, name="ww%d" % u, align_bytes=64)
-                ws = const.tile([P, 512], U8, name="ws%d" % u, align_bytes=64)
-                nc.vector.quantize_mx(
-                    out=ww[:].bitcast(FP8X4), scales=ws[:], in_=wg[:].rearrange("p n t -> p (n t)")
-                )
-                wws.append((ww, ws))
-            osb = opool.tile([P, 4, NT, HD], F32, tag="osb")
+        def w_quant(u):
+            wd = CHUNKS[u // NG][2]
+            ww = const.tile([P, wd], U32, name="ww%d" % u, align_bytes=64)
+            ws = const.tile([P, wd], U8, name="ws%d" % u, align_bytes=64)
+            nc.vector.quantize_mx(
+                out=ww[:].bitcast(FP8X4), scales=ws[:], in_=wgs[u][:].rearrange("p n t -> p (n t)")
+            )
+            wws.append((ww, ws))
+
+        def passes(u):
+            c, gg = u // NG, u % NG
+            wd = CHUNKS[c][2]
+            if gg == 0:
+                accs.append([psum.tile([P, wd], F32, tag="bank", name="acc%d_%d" % (c, j)) for j in range(NT)])
             for j in range(NT):
-                acc = psum.tile([P, 512], F32, tag="bank", name="acc")
-                for gg in range(NG):
-                    nc.tensor.matmul_mx(
-                        out=acc[:],
-                        lhsT=hw[:, j, P * gg : P * gg + P].bitcast(FP8X4),
-                        lhsT_scale=hs[:, j, P * gg : P * gg + P],
-                        rhs=wws[gg][0][:].bitcast(FP8X4),
-                        rhs_scale=wws[gg][1][:],
-                        start=(gg == 0),
-                        stop=(gg == NG - 1),
-                    )
+                nc.tensor.matmul_mx(
+                    out=accs[c][j][:],
+                    lhsT=hw[:, j, P * gg : P * gg + P].bitcast(FP8X4),
+                    lhsT_scale=hs[:, j, P * gg : P * gg + P],
+                    rhs=wws[u][0][:].bitcast(FP8X4),
+                    rhs_scale=wws[u][1][:],
+                    start=(gg == 0),
+                    stop=(gg == NG - 1),
+                )
+
+        def flush_passes():
+            if state["hq"] == NT:
+                while state["passes"] < len(wws):
+                    passes(state["passes"])
+                    state["passes"] = state["passes"] + 1
+
+        def rope_store(c):
+            m, n0, wd = CHUNKS[c]
+            om = out_0 if m == 0 else out_1
+            nh = wd // HD
+            h0 = n0 // HD
+            osb = const.tile([P, nh, NT, HD], F32, name="osb%d" % c)
+            for j in range(NT):
                 nc.vector.tensor_tensor(
                     out=osb[:, :, j, :],
-                    in0=acc[:].rearrange("p (n d) -> p n d", d=HD),
-                    in1=ctab[:, j, :, :].rearrange("p i e -> p (i e)").unsqueeze(1).to_broadcast([P, 4, HD]),
+                    in0=accs[c][j][:].rearrange("p (n d) -> p n d", d=HD),
+                    in1=ctab[:, j, :, :].rearrange("p i e -> p (i e)").unsqueeze(1).to_broadcast([P, nh, HD]),
                     op=ALU.mult,
                 )
             for b in range(B):
                 nc.sync.dma_start(
-                    out=om[b, h0 : h0 + 4, :, :].rearrange("n (lh j) d -> lh n (j d)", j=NT),
+                    out=om[b, h0 : h0 + nh, :, :].rearrange("n (lh j) d -> lh n (j d)", j=NT),
                     in_=osb[b:P:4, :, :, :].rearrange("p n j d -> p n (j d)"),
                 )
+
+        pipe = [("rv", 0)]
+        for u in range(nu):
+            if u + 1 < nu:
+                pipe.append(("rv", u + 1))
+            pipe.append(("wq", u))
+            if u >= 2 and u % 2 == 0:
+                pipe.append(("rope", (u - 2) // 2))
+        pipe.append(("rope", len(CHUNKS) - 1))
+
+        for k in range(len(pipe)):
+            while state["hq"] < NT and HQ_POS[state["hq"]] <= k:
+                h_quant(state["hq"])
+                state["hq"] = state["hq"] + 1
+                flush_passes()
+            kind, arg = pipe[k]
+            if kind == "rv":
+                regroup_v(arg)
+            elif kind == "wq":
+                w_quant(arg)
+                flush_passes()
+            else:
+                rope_store(arg)

@@ -59,15 +59,23 @@ def tile_llamaselfattentionblock_pa_kernel(tc, x, g, wq, wk, out_0, out_1):
                 wr.append(wt)
 
         ones = const.tile([P, P], BF16)
-        nc.vector.memset(ones[:], 1.0)
+        nc.gpsimd.memset(ones[:], 1.0)
         neghalf = const.tile([P, 1], F32)
-        nc.vector.memset(neghalf[:], -0.5)
+        nc.gpsimd.memset(neghalf[:], -0.5)
         warm = const.tile([P, 1], F32)
         nc.scalar.activation(out=warm[:], in_=neghalf[:], func=ACT.Sin)
-        pidx = const.tile([P, 1], I32)
-        nc.gpsimd.iota(pidx[:], pattern=[[0, 1]], base=0, channel_multiplier=1)
-        colsi = const.tile([P, P], I32)
-        nc.gpsimd.iota(colsi[:], pattern=[[1, P]], base=0, channel_multiplier=0)
+        pj = const.tile([P, NT], I32)
+        nc.gpsimd.iota(pj[:], pattern=[[0, NT]], base=0, channel_multiplier=1)
+        jj = const.tile([P, NT], I32)
+        nc.gpsimd.iota(jj[:], pattern=[[1, NT]], base=0, channel_multiplier=0)
+        pdiff = const.tile([P, 32, B], F32)
+        nc.gpsimd.iota(
+            pdiff[:], pattern=[[1, 32], [32, B]], base=0, channel_multiplier=-1, allow_small_or_imprecise_dtypes=True
+        )
+        perm = const.tile([P, P], BF16)
+        nc.gpsimd.tensor_scalar(
+            out=perm[:], in0=pdiff[:].rearrange("p l b -> p (l b)"), scalar1=0.0, scalar2=None, op0=ALU.is_equal
+        )
 
         th = const.tile([P, 64], F32)
         nc.vector.memset(th[:, 0:1], 1.0)
@@ -77,29 +85,17 @@ def tile_llamaselfattentionblock_pa_kernel(tc, x, g, wq, wk, out_0, out_1):
             nc.vector.tensor_scalar(
                 out=th[:, wd : 2 * wd], in0=th[:, 0:wd], scalar1=ratio**wd, scalar2=None, op0=ALU.mult
             )
-        jt = const.tile([P, NT, 64], F32)
+        l0i = const.tile([P, NT], I32)
+        nc.vector.tensor_scalar(out=l0i[:], in0=pj[:], scalar1=124, scalar2=None, op0=ALU.bitwise_and)
+        lji = const.tile([P, NT], I32)
+        nc.vector.tensor_tensor(out=lji[:], in0=l0i[:], in1=jj[:], op=ALU.bitwise_or)
+        ljt = const.tile([P, NT], F32)
+        nc.vector.tensor_scalar(out=ljt[:], in0=lji[:], scalar1=TURN, scalar2=None, op0=ALU.mult)
+        yy = const.tile([P, NT, 64], F32)
         for j in range(NT):
             nc.vector.tensor_scalar(
-                out=jt[:, j, :], in0=th[:], scalar1=j * TURN, scalar2=0.25, op0=ALU.mult, op1=ALU.add
+                out=yy[:, j, :], in0=th[:], scalar1=ljt[:, j : j + 1], scalar2=0.25, op0=ALU.mult, op1=ALU.add
             )
-        pa = const.tile([P, 1], I32)
-        nc.vector.tensor_scalar(
-            out=pa[:], in0=pidx[:], scalar1=31, scalar2=2, op0=ALU.bitwise_and, op1=ALU.logical_shift_left
-        )
-        pb = const.tile([P, 1], I32)
-        nc.vector.tensor_scalar(out=pb[:], in0=pidx[:], scalar1=5, scalar2=None, op0=ALU.logical_shift_right)
-        pm = const.tile([P, 1], I32)
-        nc.vector.tensor_tensor(out=pm[:], in0=pa[:], in1=pb[:], op=ALU.bitwise_or)
-        pmf = const.tile([P, 1], F32)
-        nc.vector.tensor_copy(out=pmf[:], in_=pm[:])
-        colsf = const.tile([P, P], F32)
-        nc.vector.tensor_copy(out=colsf[:], in_=colsi[:])
-        perm = const.tile([P, P], BF16)
-        nc.vector.tensor_scalar(out=perm[:], in0=colsf[:], scalar1=pmf[:, 0:1], scalar2=None, op0=ALU.is_equal)
-        l0i = const.tile([P, 1], I32)
-        nc.vector.tensor_scalar(out=l0i[:], in0=pidx[:], scalar1=124, scalar2=None, op0=ALU.bitwise_and)
-        l0f = const.tile([P, 1], F32)
-        nc.vector.tensor_scalar(out=l0f[:], in0=l0i[:], scalar1=TURN, scalar2=None, op0=ALU.mult)
 
         gps = []
         for hf in range(2):
@@ -107,25 +103,6 @@ def tile_llamaselfattentionblock_pa_kernel(tc, x, g, wq, wk, out_0, out_1):
             nc.tensor.matmul(out=gp[:], lhsT=ones[:], rhs=grow[:, 512 * hf : 512 * hf + 512], start=True, stop=True)
             gps.append(gp)
 
-        yy = const.tile([P, NT, 64], F32)
-        nc.vector.scalar_tensor_tensor(
-            out=yy[:],
-            in0=th[:].unsqueeze(1).to_broadcast([P, NT, 64]),
-            scalar=l0f[:, 0:1],
-            in1=jt[:],
-            op0=ALU.mult,
-            op1=ALU.add,
-        )
-        yi = const.tile([P, NT, 64], I32)
-        nc.vector.tensor_copy(out=yi[:], in_=yy[:])
-        yf = const.tile([P, NT, 64], F32)
-        nc.vector.tensor_copy(out=yf[:], in_=yi[:])
-        rr = const.tile([P, NT, 64], F32)
-        nc.vector.tensor_tensor(out=rr[:], in0=yy[:], in1=yf[:], op=ALU.subtract)
-        nr = const.tile([P, NT, 64], F32)
-        nc.vector.scalar_tensor_tensor(
-            out=nr[:], in0=rr[:], scalar=0.5, in1=rr[:], op0=ALU.is_gt, op1=ALU.subtract
-        )
         rstds = []
         for j in range(NT):
             me = const.tile([P, 1], F32, name="me%d" % j)
@@ -157,6 +134,16 @@ def tile_llamaselfattentionblock_pa_kernel(tc, x, g, wq, wk, out_0, out_1):
             nc.gpsimd.tensor_tensor(out=rstd[:], in0=me[:], in1=neghalf[:], op=ALU.pow)
             rstds.append(rstd)
 
+        yi = const.tile([P, NT, 64], I32)
+        nc.vector.tensor_copy(out=yi[:], in_=yy[:])
+        yf = const.tile([P, NT, 64], F32)
+        nc.vector.tensor_copy(out=yf[:], in_=yi[:])
+        rr = const.tile([P, NT, 64], F32)
+        nc.vector.tensor_tensor(out=rr[:], in0=yy[:], in1=yf[:], op=ALU.subtract)
+        nr = const.tile([P, NT, 64], F32)
+        nc.vector.scalar_tensor_tensor(
+            out=nr[:], in0=rr[:], scalar=0.5, in1=rr[:], op0=ALU.is_gt, op1=ALU.subtract
+        )
         ctab = const.tile([P, NT, 64, 2], F32)
         nc.scalar.activation(
             out=ctab[:],

@@ -20,21 +20,17 @@ NT = 4
 NG = 2
 TURN = 1.0 / (2.0 * math.pi)
 CHUNKS = [(0, 0, 512), (0, 512, 512), (1, 0, 512), (1, 512, 256), (1, 768, 256)]
-VCOLS = [288, 320, 192, 160, 0, 0, 0, 96, 0, 0]
+VCOLS = {(0, 0): 256, (0, 1): 512, (1, 0): 256}
 SPLIT_STATS = [True, True, False, False]
-S_PRE = 2
-HQ_POS = [2, 3, 4, 4]
-PIN = True
 
 
 def tile_llamaselfattentionblock_pa_kernel(tc, x, g, wq, wk, out_0, out_1):
     nc = tc.nc
-    nu = NG * len(CHUNKS)
+    nch = len(CHUNKS)
     with ExitStack() as ctx:
         const = ctx.enter_context(tc.tile_pool(name="const", bufs=1))
         psum = ctx.enter_context(tc.psum_pool(name="psum", bufs=8))
-        if PIN:
-            ctx.enter_context(tc.manual_schedule())
+        ctx.enter_context(tc.manual_schedule())
 
         grow = const.tile([P, E], BF16)
         nc.vector.memset(grow[:], 0.0)
@@ -47,16 +43,16 @@ def tile_llamaselfattentionblock_pa_kernel(tc, x, g, wq, wk, out_0, out_1):
             if j == 0:
                 nc.sync.dma_start(out=grow[0:1, :], in_=g.rearrange("(o k) -> o k", o=1))
         wr = []
-        for c in range(len(CHUNKS)):
+        for c in range(nch):
             m, n0, wd = CHUNKS[c]
             w = wq if m == 0 else wk
+            wt = const.tile([P, NG, 4, wd], BF16, name="wr%d" % c)
             for gg in range(NG):
-                wt = const.tile([P, 4, wd], BF16, name="wr%d" % (c * NG + gg))
                 nc.sync.dma_start(
-                    out=wt[:],
+                    out=wt[:, gg, :, :],
                     in_=w[512 * gg : 512 * gg + 512, n0 : n0 + wd].rearrange("(t p) n -> p t n", p=P),
                 )
-                wr.append(wt)
+            wr.append(wt)
 
         ones = const.tile([P, P], BF16)
         nc.gpsimd.memset(ones[:], 1.0)
@@ -97,11 +93,10 @@ def tile_llamaselfattentionblock_pa_kernel(tc, x, g, wq, wk, out_0, out_1):
                 out=yy[:, j, :], in0=th[:], scalar1=ljt[:, j : j + 1], scalar2=0.25, op0=ALU.mult, op1=ALU.add
             )
 
-        gps = []
+        gp = psum.tile([P, E], BF16, tag="bank", name="gp")
         for hf in range(2):
-            gp = psum.tile([P, 512], F32, tag="bank", name="gp%d" % hf)
-            nc.tensor.matmul(out=gp[:], lhsT=ones[:], rhs=grow[:, 512 * hf : 512 * hf + 512], start=True, stop=True)
-            gps.append(gp)
+            sl = slice(512 * hf, 512 * hf + 512)
+            nc.tensor.matmul(out=gp[:, sl], lhsT=ones[:], rhs=grow[:, sl], start=True, stop=True)
 
         rstds = []
         for j in range(NT):
@@ -155,56 +150,45 @@ def tile_llamaselfattentionblock_pa_kernel(tc, x, g, wq, wk, out_0, out_1):
         tps = []
         for j in range(NT):
             hj = const.tile([P, E], BF16, name="h%d" % j)
-            for hf in range(2):
-                sl = slice(512 * hf, 512 * hf + 512)
-                nc.vector.scalar_tensor_tensor(
-                    out=hj[:, sl],
-                    in0=xt[j][:, sl],
-                    scalar=rstds[j][:, 0:1],
-                    in1=gps[hf][:],
-                    op0=ALU.mult,
-                    op1=ALU.mult,
-                )
+            nc.vector.scalar_tensor_tensor(
+                out=hj[:], in0=xt[j][:], scalar=rstds[j][:, 0:1], in1=gp[:], op0=ALU.mult, op1=ALU.mult
+            )
             tp = psum.tile([P, 8, P], BF16, tag="bank", name="tp%d" % j)
             for q in range(8):
                 nc.tensor.transpose(out=tp[:, q, :], in_=hj[:, P * q : P * q + P], identity=perm[:])
             tps.append(tp)
 
-        wgs = []
-        for u in range(nu):
-            wd = CHUNKS[u // NG][2]
-            wgs.append(const.tile([P, wd, 4], BF16, name="wg%d" % u, align_bytes=64))
+        wgs = [const.tile([P, NG, CHUNKS[c][2], 4], BF16, name="wg%d" % c, align_bytes=64) for c in range(nch)]
 
-        def regroup(eng_copy, u, c0, c1):
+        def regroup(eng_copy, c, gg, c0, c1):
             eng_copy(
-                out=wgs[u][:, c0:c1, :].rearrange("p (c i) t -> p c t i", i=4),
-                in_=wr[u][:, :, c0:c1].rearrange("p t (c i) -> p c t i", i=4),
+                out=wgs[c][:, gg, c0:c1, :].rearrange("p (c i) t -> p c t i", i=4),
+                in_=wr[c][:, gg, :, c0:c1].rearrange("p t (c i) -> p c t i", i=4),
             )
 
-        def regroup_s(u):
-            wd = CHUNKS[u // NG][2]
-            if VCOLS[u] < wd:
-                regroup(nc.scalar.copy, u, VCOLS[u], wd)
+        def regroup_s(c, gg):
+            if VCOLS.get((c, gg), 0) < CHUNKS[c][2]:
+                regroup(nc.scalar.copy, c, gg, VCOLS.get((c, gg), 0), CHUNKS[c][2])
 
-        def regroup_v(u):
-            if VCOLS[u] > 0:
-                regroup(nc.vector.tensor_copy, u, 0, VCOLS[u])
+        def regroup_v(c, gg):
+            regroup(nc.vector.tensor_copy, c, gg, 0, VCOLS[(c, gg)])
 
-        for u in range(S_PRE):
-            regroup_s(u)
+        regroup_s(0, 0)
         hgs = []
         for j in range(NT):
             hg = const.tile([P, NG, P, 4], BF16, name="hg%d" % j, align_bytes=64)
             nc.scalar.copy(out=hg[:], in_=tps[j][:].rearrange("p (g t) l -> p g l t", t=4))
             hgs.append(hg)
-        for u in range(S_PRE, nu):
-            regroup_s(u)
+        for c in range(nch):
+            for gg in range(NG):
+                if (c, gg) != (0, 0):
+                    regroup_s(c, gg)
 
-        hw = const.tile([P, NT, 256], U32, align_bytes=64)
-        hs = const.tile([P, NT, 256], U8, align_bytes=64)
-        wws = []
-        accs = []
-        state = {"hq": 0, "passes": 0}
+        hw = const.tile([P, NT, NG * P], U32, align_bytes=64)
+        hs = const.tile([P, NT, NG * P], U8, align_bytes=64)
+        wws = [const.tile([P, NG, CHUNKS[c][2]], U32, name="ww%d" % c, align_bytes=64) for c in range(nch)]
+        wss = [const.tile([P, NG, CHUNKS[c][2]], U8, name="ws%d" % c, align_bytes=64) for c in range(nch)]
+        accs = {}
 
         def h_quant(j):
             nc.vector.quantize_mx(
@@ -213,36 +197,42 @@ def tile_llamaselfattentionblock_pa_kernel(tc, x, g, wq, wk, out_0, out_1):
                 in_=hgs[j][:].rearrange("p g l t -> p (g l t)"),
             )
 
-        def w_quant(u):
-            wd = CHUNKS[u // NG][2]
-            ww = const.tile([P, wd], U32, name="ww%d" % u, align_bytes=64)
-            ws = const.tile([P, wd], U8, name="ws%d" % u, align_bytes=64)
+        def w_quant(c, gg):
             nc.vector.quantize_mx(
-                out=ww[:].bitcast(FP8X4), scales=ws[:], in_=wgs[u][:].rearrange("p n t -> p (n t)")
+                out=wws[c][:, gg, :].bitcast(FP8X4),
+                scales=wss[c][:, gg, :],
+                in_=wgs[c][:, gg, :, :].rearrange("p n t -> p (n t)"),
             )
-            wws.append((ww, ws))
 
-        def passes(u):
-            c, gg = u // NG, u % NG
-            wd = CHUNKS[c][2]
+        def w_quant_both(c):
+            nc.vector.quantize_mx(
+                out=wws[c][:].rearrange("p g n -> p (g n)").bitcast(FP8X4),
+                scales=wss[c][:].rearrange("p g n -> p (g n)"),
+                in_=wgs[c][:].rearrange("p g n t -> p (g n t)"),
+            )
+
+        def one_pass(acc, c, j, gg):
+            nc.tensor.matmul_mx(
+                out=acc,
+                lhsT=hw[:, j, P * gg : P * gg + P].bitcast(FP8X4),
+                lhsT_scale=hs[:, j, P * gg : P * gg + P],
+                rhs=wws[c][:, gg, :].bitcast(FP8X4),
+                rhs_scale=wss[c][:, gg, :],
+                start=(gg == 0),
+                stop=(gg == NG - 1),
+            )
+
+        def passes_wide(c, gg):
             if gg == 0:
-                accs.append([psum.tile([P, wd], F32, tag="bank", name="acc%d_%d" % (c, j)) for j in range(NT)])
+                accs[c] = [psum.tile([P, 512], F32, tag="bank", name="acc%d_%d" % (c, j)) for j in range(NT)]
             for j in range(NT):
-                nc.tensor.matmul_mx(
-                    out=accs[c][j][:],
-                    lhsT=hw[:, j, P * gg : P * gg + P].bitcast(FP8X4),
-                    lhsT_scale=hs[:, j, P * gg : P * gg + P],
-                    rhs=wws[u][0][:].bitcast(FP8X4),
-                    rhs_scale=wws[u][1][:],
-                    start=(gg == 0),
-                    stop=(gg == NG - 1),
-                )
+                one_pass(accs[c][j][:], c, j, gg)
 
-        def flush_passes():
-            if state["hq"] == NT:
-                while state["passes"] < len(wws):
-                    passes(state["passes"])
-                    state["passes"] = state["passes"] + 1
+        def passes_narrow(c):
+            accs[c] = [psum.tile([P, 2, 256], F32, tag="bank", name="acc%d_%d" % (c, jp)) for jp in range(2)]
+            for j in range(NT):
+                for gg in range(NG):
+                    one_pass(accs[c][j // 2][:, j % 2, :], c, j, gg)
 
         def rope_store(c):
             m, n0, wd = CHUNKS[c]
@@ -250,38 +240,54 @@ def tile_llamaselfattentionblock_pa_kernel(tc, x, g, wq, wk, out_0, out_1):
             nh = wd // HD
             h0 = n0 // HD
             osb = const.tile([P, nh, NT, HD], F32, name="osb%d" % c)
-            for j in range(NT):
-                nc.vector.tensor_tensor(
-                    out=osb[:, :, j, :],
-                    in0=accs[c][j][:].rearrange("p (n d) -> p n d", d=HD),
-                    in1=ctab[:, j, :, :].rearrange("p i e -> p (i e)").unsqueeze(1).to_broadcast([P, nh, HD]),
-                    op=ALU.mult,
-                )
+            ct = ctab[:].rearrange("p j i e -> p j (i e)")
+            if wd == 512:
+                for j in range(NT):
+                    nc.vector.tensor_tensor(
+                        out=osb[:, :, j, :],
+                        in0=accs[c][j][:].rearrange("p (n d) -> p n d", d=HD),
+                        in1=ct[:, j, :].unsqueeze(1).to_broadcast([P, nh, HD]),
+                        op=ALU.mult,
+                    )
+            else:
+                for jp in range(2):
+                    nc.vector.tensor_tensor(
+                        out=osb[:, :, 2 * jp : 2 * jp + 2, :],
+                        in0=accs[c][jp][:].rearrange("p j (n d) -> p n j d", d=HD),
+                        in1=ct[:, 2 * jp : 2 * jp + 2, :].unsqueeze(1).to_broadcast([P, nh, 2, HD]),
+                        op=ALU.mult,
+                    )
             for b in range(B):
                 nc.sync.dma_start(
                     out=om[b, h0 : h0 + nh, :, :].rearrange("n (lh j) d -> lh n (j d)", j=NT),
                     in_=osb[b:P:4, :, :, :].rearrange("p n j d -> p n (j d)"),
                 )
 
-        pipe = [("rv", 0)]
-        for u in range(nu):
-            if u + 1 < nu:
-                pipe.append(("rv", u + 1))
-            pipe.append(("wq", u))
-            if u >= 2 and u % 2 == 0:
-                pipe.append(("rope", (u - 2) // 2))
-        pipe.append(("rope", len(CHUNKS) - 1))
-
-        for k in range(len(pipe)):
-            while state["hq"] < NT and HQ_POS[state["hq"]] <= k:
-                h_quant(state["hq"])
-                state["hq"] = state["hq"] + 1
-                flush_passes()
-            kind, arg = pipe[k]
-            if kind == "rv":
-                regroup_v(arg)
-            elif kind == "wq":
-                w_quant(arg)
-                flush_passes()
-            else:
-                rope_store(arg)
+        h_quant(0)
+        regroup_v(0, 0)
+        h_quant(1)
+        w_quant(0, 0)
+        h_quant(2)
+        regroup_v(0, 1)
+        h_quant(3)
+        regroup_v(1, 0)
+        passes_wide(0, 0)
+        w_quant(0, 1)
+        passes_wide(0, 1)
+        w_quant(1, 0)
+        passes_wide(1, 0)
+        rope_store(0)
+        w_quant(1, 1)
+        passes_wide(1, 1)
+        w_quant(2, 0)
+        passes_wide(2, 0)
+        rope_store(1)
+        w_quant(2, 1)
+        passes_wide(2, 1)
+        w_quant_both(3)
+        passes_narrow(3)
+        rope_store(2)
+        w_quant_both(4)
+        passes_narrow(4)
+        rope_store(3)
+        rope_store(4)

@@ -20,7 +20,8 @@ NT = 4
 NG = 2
 TURN = 1.0 / (2.0 * math.pi)
 CHUNKS = [(0, 0, 512), (0, 512, 512), (1, 0, 512), (1, 512, 256), (1, 768, 256)]
-VCOLS = {(0, 0): 256, (0, 1): 512, (1, 0): 256}
+VCOLS = {(0, 0): 256, (0, 1): 256, (1, 0): 256}
+GCOLS = {(0, 1): 256, (2, 0): 256, (3, 0): 256, (4, 0): 256}
 SPLIT_STATS = [True, True, False, False]
 
 
@@ -167,12 +168,31 @@ def tile_llamaselfattentionblock_pa_kernel(tc, x, g, wq, wk, out_0, out_1):
             )
 
         def regroup_s(c, gg):
-            if VCOLS.get((c, gg), 0) < CHUNKS[c][2]:
-                regroup(nc.scalar.copy, c, gg, VCOLS.get((c, gg), 0), CHUNKS[c][2])
+            c1 = CHUNKS[c][2] - GCOLS.get((c, gg), 0)
+            if VCOLS.get((c, gg), 0) < c1:
+                regroup(nc.scalar.copy, c, gg, VCOLS.get((c, gg), 0), c1)
+
+        def regroup_g(c, gg, one):
+            c1 = CHUNKS[c][2]
+            for c0 in range(c1 - GCOLS[(c, gg)], c1, P):
+                nc.gpsimd.tensor_scalar(
+                    out=wgs[c][:, gg, c0 : c0 + P, :],
+                    in0=wr[c][:, gg, :, c0 : c0 + P].rearrange("p t n -> p n t"),
+                    scalar1=one,
+                    scalar2=0.0,
+                    op0=ALU.mult,
+                    op1=ALU.add,
+                )
+
+        def gate(k):
+            one = const.tile([P, 1], F32, name="one%d" % k)
+            nc.vector.memset(one[:], 1.0)
+            return one[:, 0:1]
 
         def regroup_v(c, gg):
             regroup(nc.vector.tensor_copy, c, gg, 0, VCOLS[(c, gg)])
 
+        regroup_g(0, 1, 1.0)
         regroup_s(0, 0)
         hgs = []
         for j in range(NT):
@@ -276,16 +296,19 @@ def tile_llamaselfattentionblock_pa_kernel(tc, x, g, wq, wk, out_0, out_1):
         passes_wide(0, 1)
         w_quant(1, 0)
         passes_wide(1, 0)
+        regroup_g(2, 0, gate(0))
         rope_store(0)
         w_quant(1, 1)
         passes_wide(1, 1)
         w_quant(2, 0)
         passes_wide(2, 0)
+        regroup_g(3, 0, gate(1))
         rope_store(1)
         w_quant(2, 1)
         passes_wide(2, 1)
         w_quant_both(3)
         passes_narrow(3)
+        regroup_g(4, 0, gate(2))
         rope_store(2)
         w_quant_both(4)
         passes_narrow(4)

@@ -13,304 +13,312 @@ ALU = mybir.AluOpType
 ACT = mybir.ActivationFunctionType
 
 P = 128
-B, L, E, H, HD = 4, 128, 1024, 8, 128
+PACK = 4
+PASSES = 2
+BATCH, POSITIONS, EMBED, HEADS, HEAD_DIM = 4, 128, 1024, 8, 128
+TILES = 4
+PAIRS = HEAD_DIM // 2
 EPS = 1e-6
-FLOPS = 2 * B * L * E * 2 * H * HD
-NT = 4
-NG = 2
 TURN = 1.0 / (2.0 * math.pi)
+FLOPS = 2 * BATCH * POSITIONS * EMBED * 2 * HEADS * HEAD_DIM
+
 CHUNKS = [(0, 0, 512), (0, 512, 512), (1, 0, 512), (1, 512, 256), (1, 768, 256)]
-VCOLS = {(0, 0): 256, (0, 1): 256, (1, 0): 256}
-GCOLS = {(0, 1): 256, (2, 0): 256, (3, 0): 256, (4, 0): 256}
-SPLIT_STATS = [True, True, False, False]
+VECTOR_COLS = {(0, 0): 256, (0, 1): 256, (1, 0): 256}
+GPSIMD_COLS = {(0, 1): 256, (2, 0): 256, (3, 0): 256, (4, 0): 256}
+HALVED_TILES = 2
 
 
 def tile_llamaselfattentionblock_pa_kernel(tc, x, g, wq, wk, out_0, out_1):
     nc = tc.nc
-    nch = len(CHUNKS)
+    n_chunks = len(CHUNKS)
     with ExitStack() as ctx:
-        const = ctx.enter_context(tc.tile_pool(name="const", bufs=1))
+        sbuf = ctx.enter_context(tc.tile_pool(name="sbuf", bufs=1))
         psum = ctx.enter_context(tc.psum_pool(name="psum", bufs=8))
         ctx.enter_context(tc.manual_schedule())
 
-        grow = const.tile([P, E], BF16)
-        nc.vector.memset(grow[:], 0.0)
-        xv = x.rearrange("b l k -> (b l) k").rearrange("(p j) k -> p j k", j=NT)
-        xt = []
-        for j in range(NT):
-            xj = const.tile([P, E], BF16, name="x%d" % j)
-            nc.sync.dma_start(out=xj[:], in_=xv[:, j, :])
-            xt.append(xj)
+        g_row = sbuf.tile([P, EMBED], BF16)
+        nc.vector.memset(g_row[:], 0.0)
+        x_tiles_dram = x.rearrange("b l k -> (b l) k").rearrange("(i j) k -> i j k", j=TILES)
+        x_tiles = []
+        for j in range(TILES):
+            x_j = sbuf.tile([P, EMBED], BF16, name="x%d" % j)
+            nc.sync.dma_start(out=x_j[:], in_=x_tiles_dram[:, j, :])
+            x_tiles.append(x_j)
             if j == 0:
-                nc.sync.dma_start(out=grow[0:1, :], in_=g.rearrange("(o k) -> o k", o=1))
-        wr = []
-        for c in range(nch):
-            m, n0, wd = CHUNKS[c]
-            w = wq if m == 0 else wk
-            wt = const.tile([P, NG, 4, wd], BF16, name="wr%d" % c)
-            for gg in range(NG):
+                nc.sync.dma_start(out=g_row[0:1, :], in_=g.rearrange("(o k) -> o k", o=1))
+        w_rows = []
+        for c in range(n_chunks):
+            which, first, width = CHUNKS[c]
+            w = wq if which == 0 else wk
+            w_c = sbuf.tile([P, PASSES, PACK, width], BF16, name="w_rows%d" % c)
+            for u in range(PASSES):
+                k0 = P * PACK * u
                 nc.sync.dma_start(
-                    out=wt[:, gg, :, :],
-                    in_=w[512 * gg : 512 * gg + 512, n0 : n0 + wd].rearrange("(t p) n -> p t n", p=P),
+                    out=w_c[:, u, :, :],
+                    in_=w[k0 : k0 + P * PACK, first : first + width].rearrange("(t p) n -> p t n", p=P),
                 )
-            wr.append(wt)
+            w_rows.append(w_c)
 
-        ones = const.tile([P, P], BF16)
+        ones = sbuf.tile([P, P], BF16)
         nc.gpsimd.memset(ones[:], 1.0)
-        neghalf = const.tile([P, 1], F32)
-        nc.gpsimd.memset(neghalf[:], -0.5)
-        warm = const.tile([P, 1], F32)
-        nc.scalar.activation(out=warm[:], in_=neghalf[:], func=ACT.Sin)
-        pj = const.tile([P, NT], I32)
-        nc.gpsimd.iota(pj[:], pattern=[[0, NT]], base=0, channel_multiplier=1)
-        jj = const.tile([P, NT], I32)
-        nc.gpsimd.iota(jj[:], pattern=[[1, NT]], base=0, channel_multiplier=0)
-        pdiff = const.tile([P, 32, B], F32)
+        minus_half = sbuf.tile([P, 1], F32)
+        nc.gpsimd.memset(minus_half[:], -0.5)
+        table_warmer = sbuf.tile([P, 1], F32)
+        nc.scalar.activation(out=table_warmer[:], in_=minus_half[:], func=ACT.Sin)
+        partition_index = sbuf.tile([P, TILES], I32)
+        nc.gpsimd.iota(partition_index[:], pattern=[[0, TILES]], base=0, channel_multiplier=1)
+        tile_index = sbuf.tile([P, TILES], I32)
+        nc.gpsimd.iota(tile_index[:], pattern=[[1, TILES]], base=0, channel_multiplier=0)
+        source_minus_row = sbuf.tile([P, POSITIONS // TILES, BATCH], F32)
         nc.gpsimd.iota(
-            pdiff[:], pattern=[[1, 32], [32, B]], base=0, channel_multiplier=-1, allow_small_or_imprecise_dtypes=True
+            source_minus_row[:],
+            pattern=[[1, POSITIONS // TILES], [POSITIONS // TILES, BATCH]],
+            base=0,
+            channel_multiplier=-1,
+            allow_small_or_imprecise_dtypes=True,
         )
-        perm = const.tile([P, P], BF16)
+        permutation = sbuf.tile([P, P], BF16)
         nc.gpsimd.tensor_scalar(
-            out=perm[:], in0=pdiff[:].rearrange("p l b -> p (l b)"), scalar1=0.0, scalar2=None, op0=ALU.is_equal
+            out=permutation[:],
+            in0=source_minus_row[:].rearrange("i lh b -> i (lh b)"),
+            scalar1=0.0,
+            scalar2=None,
+            op0=ALU.is_equal,
         )
 
-        th = const.tile([P, 64], F32)
-        nc.vector.memset(th[:, 0:1], 1.0)
-        ratio = 10000.0 ** (-1.0 / 64.0)
-        for s in range(6):
-            wd = 1 << s
+        theta = sbuf.tile([P, PAIRS], F32)
+        nc.vector.memset(theta[:, 0:1], 1.0)
+        for doubling in range(6):
+            known = 1 << doubling
             nc.vector.tensor_scalar(
-                out=th[:, wd : 2 * wd], in0=th[:, 0:wd], scalar1=ratio**wd, scalar2=None, op0=ALU.mult
+                out=theta[:, known : 2 * known],
+                in0=theta[:, 0:known],
+                scalar1=10000.0 ** (-known / 64.0),
+                scalar2=None,
+                op0=ALU.mult,
             )
-        l0i = const.tile([P, NT], I32)
-        nc.vector.tensor_scalar(out=l0i[:], in0=pj[:], scalar1=124, scalar2=None, op0=ALU.bitwise_and)
-        lji = const.tile([P, NT], I32)
-        nc.vector.tensor_tensor(out=lji[:], in0=l0i[:], in1=jj[:], op=ALU.bitwise_or)
-        ljt = const.tile([P, NT], F32)
-        nc.vector.tensor_scalar(out=ljt[:], in0=lji[:], scalar1=TURN, scalar2=None, op0=ALU.mult)
-        yy = const.tile([P, NT, 64], F32)
-        for j in range(NT):
+        position_base = sbuf.tile([P, TILES], I32)
+        nc.vector.tensor_scalar(
+            out=position_base[:], in0=partition_index[:], scalar1=124, scalar2=None, op0=ALU.bitwise_and
+        )
+        position = sbuf.tile([P, TILES], I32)
+        nc.vector.tensor_tensor(out=position[:], in0=position_base[:], in1=tile_index[:], op=ALU.bitwise_or)
+        position_turns = sbuf.tile([P, TILES], F32)
+        nc.vector.tensor_scalar(out=position_turns[:], in0=position[:], scalar1=TURN, scalar2=None, op0=ALU.mult)
+        turns = sbuf.tile([P, TILES, PAIRS], F32)
+        for j in range(TILES):
             nc.vector.tensor_scalar(
-                out=yy[:, j, :], in0=th[:], scalar1=ljt[:, j : j + 1], scalar2=0.25, op0=ALU.mult, op1=ALU.add
+                out=turns[:, j, :],
+                in0=theta[:],
+                scalar1=position_turns[:, j : j + 1],
+                scalar2=0.25,
+                op0=ALU.mult,
+                op1=ALU.add,
             )
 
-        gp = psum.tile([P, E], BF16, tag="bank", name="gp")
-        for hf in range(2):
-            sl = slice(512 * hf, 512 * hf + 512)
-            nc.tensor.matmul(out=gp[:, sl], lhsT=ones[:], rhs=grow[:, sl], start=True, stop=True)
+        g_all = psum.tile([P, EMBED], BF16, tag="bank")
+        for half in range(2):
+            cols = slice(512 * half, 512 * half + 512)
+            nc.tensor.matmul(out=g_all[:, cols], lhsT=ones[:], rhs=g_row[:, cols], start=True, stop=True)
 
-        rstds = []
-        for j in range(NT):
-            me = const.tile([P, 1], F32, name="me%d" % j)
-            msa = const.tile([P, 1], F32, name="msa%d" % j)
-            if SPLIT_STATS[j]:
-                junka = const.tile([P, 512], BF16, name="junka%d" % j)
+        rstd = []
+        for j in range(TILES):
+            mean_eps = sbuf.tile([P, 1], F32, name="mean_eps%d" % j)
+            mean_a = sbuf.tile([P, 1], F32, name="mean_a%d" % j)
+            if j < HALVED_TILES:
+                squares_a = sbuf.tile([P, EMBED // 2], BF16, name="squares_a%d" % j)
                 nc.scalar.activation(
-                    out=junka[:], in_=xt[j][:, 0:512], func=ACT.Square, scale=1.0 / 32.0, accum_out=msa[:]
+                    out=squares_a[:],
+                    in_=x_tiles[j][:, 0 : EMBED // 2],
+                    func=ACT.Square,
+                    scale=1.0 / 32.0,
+                    accum_out=mean_a[:],
                 )
-                junkb = const.tile([P, 512], F32, name="junkb%d" % j)
-                msb = const.tile([P, 1], F32, name="msb%d" % j)
+                squares_b = sbuf.tile([P, EMBED // 2], F32, name="squares_b%d" % j)
+                mean_b = sbuf.tile([P, 1], F32, name="mean_b%d" % j)
                 nc.vector.scalar_tensor_tensor(
-                    out=junkb[:],
-                    in0=xt[j][:, 512:1024],
+                    out=squares_b[:],
+                    in0=x_tiles[j][:, EMBED // 2 : EMBED],
                     scalar=1.0 / 1024.0,
-                    in1=xt[j][:, 512:1024],
+                    in1=x_tiles[j][:, EMBED // 2 : EMBED],
                     op0=ALU.mult,
                     op1=ALU.mult,
-                    accum_out=msb[:],
+                    accum_out=mean_b[:],
                 )
                 nc.gpsimd.tensor_scalar(
-                    out=me[:], in0=msa[:], scalar1=msb[:, 0:1], scalar2=EPS, op0=ALU.add, op1=ALU.add
+                    out=mean_eps[:], in0=mean_a[:], scalar1=mean_b[:, 0:1], scalar2=EPS, op0=ALU.add, op1=ALU.add
                 )
             else:
-                junka = const.tile([P, E], BF16, name="junka%d" % j)
-                nc.scalar.activation(out=junka[:], in_=xt[j][:], func=ACT.Square, scale=1.0 / 32.0, accum_out=msa[:])
-                nc.gpsimd.tensor_scalar(out=me[:], in0=msa[:], scalar1=1.0, scalar2=EPS, op0=ALU.mult, op1=ALU.add)
-            rstd = const.tile([P, 1], F32, name="rstd%d" % j)
-            nc.gpsimd.tensor_tensor(out=rstd[:], in0=me[:], in1=neghalf[:], op=ALU.pow)
-            rstds.append(rstd)
+                squares_a = sbuf.tile([P, EMBED], BF16, name="squares_a%d" % j)
+                nc.scalar.activation(
+                    out=squares_a[:], in_=x_tiles[j][:], func=ACT.Square, scale=1.0 / 32.0, accum_out=mean_a[:]
+                )
+                nc.gpsimd.tensor_scalar(
+                    out=mean_eps[:], in0=mean_a[:], scalar1=1.0, scalar2=EPS, op0=ALU.mult, op1=ALU.add
+                )
+            rstd_j = sbuf.tile([P, 1], F32, name="rstd%d" % j)
+            nc.gpsimd.tensor_tensor(out=rstd_j[:], in0=mean_eps[:], in1=minus_half[:], op=ALU.pow)
+            rstd.append(rstd_j)
 
-        yi = const.tile([P, NT, 64], I32)
-        nc.vector.tensor_copy(out=yi[:], in_=yy[:])
-        yf = const.tile([P, NT, 64], F32)
-        nc.vector.tensor_copy(out=yf[:], in_=yi[:])
-        rr = const.tile([P, NT, 64], F32)
-        nc.vector.tensor_tensor(out=rr[:], in0=yy[:], in1=yf[:], op=ALU.subtract)
-        nr = const.tile([P, NT, 64], F32)
+        whole_turns_int = sbuf.tile([P, TILES, PAIRS], I32)
+        nc.vector.tensor_copy(out=whole_turns_int[:], in_=turns[:])
+        whole_turns = sbuf.tile([P, TILES, PAIRS], F32)
+        nc.vector.tensor_copy(out=whole_turns[:], in_=whole_turns_int[:])
+        rest = sbuf.tile([P, TILES, PAIRS], F32)
+        nc.vector.tensor_tensor(out=rest[:], in0=turns[:], in1=whole_turns[:], op=ALU.subtract)
+        minus_rest = sbuf.tile([P, TILES, PAIRS], F32)
         nc.vector.scalar_tensor_tensor(
-            out=nr[:], in0=rr[:], scalar=0.5, in1=rr[:], op0=ALU.is_gt, op1=ALU.subtract
+            out=minus_rest[:], in0=rest[:], scalar=0.5, in1=rest[:], op0=ALU.is_gt, op1=ALU.subtract
         )
-        ctab = const.tile([P, NT, 64, 2], F32)
+        cosines = sbuf.tile([P, TILES, PAIRS, 2], F32)
         nc.scalar.activation(
-            out=ctab[:],
-            in_=nr[:].unsqueeze(3).to_broadcast([P, NT, 64, 2]),
+            out=cosines[:],
+            in_=minus_rest[:].unsqueeze(3).to_broadcast([P, TILES, PAIRS, 2]),
             func=ACT.Sin,
             scale=-2.0 * math.pi,
         )
 
-        tps = []
-        for j in range(NT):
-            hj = const.tile([P, E], BF16, name="h%d" % j)
+        h_t = []
+        for j in range(TILES):
+            h_j = sbuf.tile([P, EMBED], BF16, name="h%d" % j)
             nc.vector.scalar_tensor_tensor(
-                out=hj[:], in0=xt[j][:], scalar=rstds[j][:, 0:1], in1=gp[:], op0=ALU.mult, op1=ALU.mult
+                out=h_j[:], in0=x_tiles[j][:], scalar=rstd[j][:, 0:1], in1=g_all[:], op0=ALU.mult, op1=ALU.mult
             )
-            tp = psum.tile([P, 8, P], BF16, tag="bank", name="tp%d" % j)
-            for q in range(8):
-                nc.tensor.transpose(out=tp[:, q, :], in_=hj[:, P * q : P * q + P], identity=perm[:])
-            tps.append(tp)
+            h_t_j = psum.tile([P, PASSES * PACK, P], BF16, tag="bank", name="h_t%d" % j)
+            for ut in range(PASSES * PACK):
+                nc.tensor.transpose(out=h_t_j[:, ut, :], in_=h_j[:, P * ut : P * ut + P], identity=permutation[:])
+            h_t.append(h_t_j)
 
-        wgs = [const.tile([P, NG, CHUNKS[c][2], 4], BF16, name="wg%d" % c, align_bytes=64) for c in range(nch)]
+        w_grouped = [
+            sbuf.tile([P, PASSES, CHUNKS[c][2], PACK], BF16, name="w_grouped%d" % c, align_bytes=64)
+            for c in range(n_chunks)
+        ]
 
-        def regroup(eng_copy, c, gg, c0, c1):
-            eng_copy(
-                out=wgs[c][:, gg, c0:c1, :].rearrange("p (c i) t -> p c t i", i=4),
-                in_=wr[c][:, gg, :, c0:c1].rearrange("p t (c i) -> p c t i", i=4),
+        def regroup(copy, c, u, n0, n1):
+            copy(
+                out=w_grouped[c][:, u, n0:n1, :].rearrange("p (run n) t -> p run t n", n=4),
+                in_=w_rows[c][:, u, :, n0:n1].rearrange("p t (run n) -> p run t n", n=4),
             )
 
-        def regroup_s(c, gg):
-            c1 = CHUNKS[c][2] - GCOLS.get((c, gg), 0)
-            if VCOLS.get((c, gg), 0) < c1:
-                regroup(nc.scalar.copy, c, gg, VCOLS.get((c, gg), 0), c1)
+        def regroup_on_vector(c, u):
+            regroup(nc.vector.tensor_copy, c, u, 0, VECTOR_COLS[(c, u)])
 
-        def regroup_g(c, gg, one):
-            c1 = CHUNKS[c][2]
-            for c0 in range(c1 - GCOLS[(c, gg)], c1, P):
+        def regroup_on_scalar(c, u):
+            n0 = VECTOR_COLS.get((c, u), 0)
+            n1 = CHUNKS[c][2] - GPSIMD_COLS.get((c, u), 0)
+            if n0 < n1:
+                regroup(nc.scalar.copy, c, u, n0, n1)
+
+        def regroup_on_gpsimd(c, u, one):
+            width = CHUNKS[c][2]
+            for n0 in range(width - GPSIMD_COLS[(c, u)], width, 128):
                 nc.gpsimd.tensor_scalar(
-                    out=wgs[c][:, gg, c0 : c0 + P, :],
-                    in0=wr[c][:, gg, :, c0 : c0 + P].rearrange("p t n -> p n t"),
+                    out=w_grouped[c][:, u, n0 : n0 + 128, :],
+                    in0=w_rows[c][:, u, :, n0 : n0 + 128].rearrange("p t n -> p n t"),
                     scalar1=one,
                     scalar2=0.0,
                     op0=ALU.mult,
                     op1=ALU.add,
                 )
 
-        def gate(k):
-            one = const.tile([P, 1], F32, name="one%d" % k)
+        def one_written_by_vector_now(c):
+            one = sbuf.tile([P, 1], F32, name="one%d" % c)
             nc.vector.memset(one[:], 1.0)
             return one[:, 0:1]
 
-        def regroup_v(c, gg):
-            regroup(nc.vector.tensor_copy, c, gg, 0, VCOLS[(c, gg)])
+        regroup_on_gpsimd(0, 1, 1.0)
 
-        regroup_g(0, 1, 1.0)
-        regroup_s(0, 0)
-        hgs = []
-        for j in range(NT):
-            hg = const.tile([P, NG, P, 4], BF16, name="hg%d" % j, align_bytes=64)
-            nc.scalar.copy(out=hg[:], in_=tps[j][:].rearrange("p (g t) l -> p g l t", t=4))
-            hgs.append(hg)
-        for c in range(nch):
-            for gg in range(NG):
-                if (c, gg) != (0, 0):
-                    regroup_s(c, gg)
+        regroup_on_scalar(0, 0)
+        h_grouped = []
+        for j in range(TILES):
+            h_grouped_j = sbuf.tile([P, PASSES, P, PACK], BF16, name="h_grouped%d" % j, align_bytes=64)
+            nc.scalar.copy(out=h_grouped_j[:], in_=h_t[j][:].rearrange("p (u t) col -> p u col t", t=PACK))
+            h_grouped.append(h_grouped_j)
+        for c in range(n_chunks):
+            for u in range(PASSES):
+                if (c, u) != (0, 0):
+                    regroup_on_scalar(c, u)
 
-        hw = const.tile([P, NT, NG * P], U32, align_bytes=64)
-        hs = const.tile([P, NT, NG * P], U8, align_bytes=64)
-        wws = [const.tile([P, NG, CHUNKS[c][2]], U32, name="ww%d" % c, align_bytes=64) for c in range(nch)]
-        wss = [const.tile([P, NG, CHUNKS[c][2]], U8, name="ws%d" % c, align_bytes=64) for c in range(nch)]
-        accs = {}
+        h_words = sbuf.tile([P, TILES, PASSES * P], U32, align_bytes=64)
+        h_scales = sbuf.tile([P, TILES, PASSES * P], U8, align_bytes=64)
+        w_words = [
+            sbuf.tile([P, PASSES, CHUNKS[c][2]], U32, name="w_words%d" % c, align_bytes=64) for c in range(n_chunks)
+        ]
+        w_scales = [
+            sbuf.tile([P, PASSES, CHUNKS[c][2]], U8, name="w_scales%d" % c, align_bytes=64) for c in range(n_chunks)
+        ]
+        sums = {}
 
-        def h_quant(j):
+        def quantise_h(j):
             nc.vector.quantize_mx(
-                out=hw[:, j, :].bitcast(FP8X4),
-                scales=hs[:, j, :],
-                in_=hgs[j][:].rearrange("p g l t -> p (g l t)"),
+                out=h_words[:, j, :].bitcast(FP8X4),
+                scales=h_scales[:, j, :],
+                in_=h_grouped[j][:].rearrange("p u col t -> p (u col t)"),
             )
 
-        def w_quant(c, gg):
+        def quantise_w(c, u):
             nc.vector.quantize_mx(
-                out=wws[c][:, gg, :].bitcast(FP8X4),
-                scales=wss[c][:, gg, :],
-                in_=wgs[c][:, gg, :, :].rearrange("p n t -> p (n t)"),
+                out=w_words[c][:, u, :].bitcast(FP8X4),
+                scales=w_scales[c][:, u, :],
+                in_=w_grouped[c][:, u, :, :].rearrange("p n t -> p (n t)"),
             )
 
-        def w_quant_both(c):
-            nc.vector.quantize_mx(
-                out=wws[c][:].rearrange("p g n -> p (g n)").bitcast(FP8X4),
-                scales=wss[c][:].rearrange("p g n -> p (g n)"),
-                in_=wgs[c][:].rearrange("p g n t -> p (g n t)"),
-            )
-
-        def one_pass(acc, c, j, gg):
-            nc.tensor.matmul_mx(
-                out=acc,
-                lhsT=hw[:, j, P * gg : P * gg + P].bitcast(FP8X4),
-                lhsT_scale=hs[:, j, P * gg : P * gg + P],
-                rhs=wws[c][:, gg, :].bitcast(FP8X4),
-                rhs_scale=wss[c][:, gg, :],
-                start=(gg == 0),
-                stop=(gg == NG - 1),
-            )
-
-        def passes_wide(c, gg):
-            if gg == 0:
-                accs[c] = [psum.tile([P, 512], F32, tag="bank", name="acc%d_%d" % (c, j)) for j in range(NT)]
-            for j in range(NT):
-                one_pass(accs[c][j][:], c, j, gg)
-
-        def passes_narrow(c):
-            accs[c] = [psum.tile([P, 2, 256], F32, tag="bank", name="acc%d_%d" % (c, jp)) for jp in range(2)]
-            for j in range(NT):
-                for gg in range(NG):
-                    one_pass(accs[c][j // 2][:, j % 2, :], c, j, gg)
-
-        def rope_store(c):
-            m, n0, wd = CHUNKS[c]
-            om = out_0 if m == 0 else out_1
-            nh = wd // HD
-            h0 = n0 // HD
-            osb = const.tile([P, nh, NT, HD], F32, name="osb%d" % c)
-            ct = ctab[:].rearrange("p j i e -> p j (i e)")
-            if wd == 512:
-                for j in range(NT):
-                    nc.vector.tensor_tensor(
-                        out=osb[:, :, j, :],
-                        in0=accs[c][j][:].rearrange("p (n d) -> p n d", d=HD),
-                        in1=ct[:, j, :].unsqueeze(1).to_broadcast([P, nh, HD]),
-                        op=ALU.mult,
-                    )
-            else:
-                for jp in range(2):
-                    nc.vector.tensor_tensor(
-                        out=osb[:, :, 2 * jp : 2 * jp + 2, :],
-                        in0=accs[c][jp][:].rearrange("p j (n d) -> p n j d", d=HD),
-                        in1=ct[:, 2 * jp : 2 * jp + 2, :].unsqueeze(1).to_broadcast([P, nh, 2, HD]),
-                        op=ALU.mult,
-                    )
-            for b in range(B):
-                nc.sync.dma_start(
-                    out=om[b, h0 : h0 + nh, :, :].rearrange("n (lh j) d -> lh n (j d)", j=NT),
-                    in_=osb[b:P:4, :, :, :].rearrange("p n j d -> p n (j d)"),
+        def multiply(c, u):
+            if u == 0:
+                sums[c] = [
+                    psum.tile([P, CHUNKS[c][2]], F32, tag="bank", name="sums%d_%d" % (c, j)) for j in range(TILES)
+                ]
+            for j in range(TILES):
+                nc.tensor.matmul_mx(
+                    out=sums[c][j][:],
+                    lhsT=h_words[:, j, P * u : P * u + P].bitcast(FP8X4),
+                    lhsT_scale=h_scales[:, j, P * u : P * u + P],
+                    rhs=w_words[c][:, u, :].bitcast(FP8X4),
+                    rhs_scale=w_scales[c][:, u, :],
+                    start=(u == 0),
+                    stop=(u == PASSES - 1),
                 )
 
-        h_quant(0)
-        regroup_v(0, 0)
-        h_quant(1)
-        w_quant(0, 0)
-        h_quant(2)
-        regroup_v(0, 1)
-        h_quant(3)
-        regroup_v(1, 0)
-        passes_wide(0, 0)
-        w_quant(0, 1)
-        passes_wide(0, 1)
-        w_quant(1, 0)
-        passes_wide(1, 0)
-        regroup_g(2, 0, gate(0))
-        rope_store(0)
-        w_quant(1, 1)
-        passes_wide(1, 1)
-        w_quant(2, 0)
-        passes_wide(2, 0)
-        regroup_g(3, 0, gate(1))
-        rope_store(1)
-        w_quant(2, 1)
-        passes_wide(2, 1)
-        w_quant_both(3)
-        passes_narrow(3)
-        regroup_g(4, 0, gate(2))
-        rope_store(2)
-        w_quant_both(4)
-        passes_narrow(4)
-        rope_store(3)
-        rope_store(4)
+        def quantise_and_multiply(c, u):
+            quantise_w(c, u)
+            multiply(c, u)
+
+        def rope_and_store(c):
+            which, first, width = CHUNKS[c]
+            out = out_0 if which == 0 else out_1
+            heads = width // HEAD_DIM
+            head0 = first // HEAD_DIM
+            result = sbuf.tile([P, heads, TILES, HEAD_DIM], F32, name="result%d" % c)
+            for j in range(TILES):
+                cosines_j = cosines[:, j, :, :].rearrange("p m twice -> p (m twice)")
+                nc.vector.tensor_tensor(
+                    out=result[:, :, j, :],
+                    in0=sums[c][j][:].rearrange("p (head d) -> p head d", d=HEAD_DIM),
+                    in1=cosines_j.unsqueeze(1).to_broadcast([P, heads, HEAD_DIM]),
+                    op=ALU.mult,
+                )
+            for b in range(BATCH):
+                nc.sync.dma_start(
+                    out=out[b, head0 : head0 + heads, :, :].rearrange("head (lh j) d -> lh head (j d)", j=TILES),
+                    in_=result[b:P:BATCH, :, :, :].rearrange("p head j d -> p head (j d)"),
+                )
+
+        quantise_h(0)
+        regroup_on_vector(0, 0)
+        quantise_h(1)
+        quantise_w(0, 0)
+        quantise_h(2)
+        regroup_on_vector(0, 1)
+        quantise_h(3)
+        regroup_on_vector(1, 0)
+        multiply(0, 0)
+        for c in range(n_chunks - 2):
+            quantise_and_multiply(c, 1)
+            quantise_and_multiply(c + 1, 0)
+            regroup_on_gpsimd(c + 2, 0, one_written_by_vector_now(c))
+            rope_and_store(c)
+        quantise_and_multiply(n_chunks - 2, 1)
+        quantise_and_multiply(n_chunks - 1, 0)
+        quantise_and_multiply(n_chunks - 1, 1)
+        rope_and_store(n_chunks - 2)
+        rope_and_store(n_chunks - 1)

import math
from contextlib import ExitStack

import concourse.mybir as mybir

FP8X4 = mybir.dt.float8_e4m3fn_x4
BF16 = mybir.dt.bfloat16
F32 = mybir.dt.float32
I32 = mybir.dt.int32
U32 = mybir.dt.uint32
U8 = mybir.dt.uint8
ALU = mybir.AluOpType
ACT = mybir.ActivationFunctionType

P = 128
PACK = 4
PASSES = 2
BATCH, POSITIONS, EMBED, HEADS, HEAD_DIM = 4, 128, 1024, 8, 128
TILES = 4
PAIRS = HEAD_DIM // 2
EPS = 1e-6
TURN = 1.0 / (2.0 * math.pi)
FLOPS = 2 * BATCH * POSITIONS * EMBED * 2 * HEADS * HEAD_DIM

CHUNKS = [(0, 0, 512), (0, 512, 512), (1, 0, 512), (1, 512, 256), (1, 768, 256)]
VECTOR_COLS = {(0, 0): 256, (0, 1): 256, (1, 0): 256}
GPSIMD_COLS = {(0, 1): 256, (2, 0): 256, (3, 0): 256, (4, 0): 256}
HALVED_TILES = 2


def tile_llamaselfattentionblock_pa_kernel(tc, x, g, wq, wk, out_0, out_1):
    nc = tc.nc
    n_chunks = len(CHUNKS)
    with ExitStack() as ctx:
        sbuf = ctx.enter_context(tc.tile_pool(name="sbuf", bufs=1))
        psum = ctx.enter_context(tc.psum_pool(name="psum", bufs=8))
        ctx.enter_context(tc.manual_schedule())

        g_row = sbuf.tile([P, EMBED], BF16)
        nc.vector.memset(g_row[:], 0.0)
        x_tiles_dram = x.rearrange("b l k -> (b l) k").rearrange("(i j) k -> i j k", j=TILES)
        x_tiles = []
        for j in range(TILES):
            x_j = sbuf.tile([P, EMBED], BF16, name="x%d" % j)
            nc.sync.dma_start(out=x_j[:], in_=x_tiles_dram[:, j, :])
            x_tiles.append(x_j)
            if j == 0:
                nc.sync.dma_start(out=g_row[0:1, :], in_=g.rearrange("(o k) -> o k", o=1))
        w_rows = []
        for c in range(n_chunks):
            which, first, width = CHUNKS[c]
            w = wq if which == 0 else wk
            w_c = sbuf.tile([P, PASSES, PACK, width], BF16, name="w_rows%d" % c)
            for u in range(PASSES):
                k0 = P * PACK * u
                nc.sync.dma_start(
                    out=w_c[:, u, :, :],
                    in_=w[k0 : k0 + P * PACK, first : first + width].rearrange("(t p) n -> p t n", p=P),
                )
            w_rows.append(w_c)

        ones = sbuf.tile([P, P], BF16)
        nc.gpsimd.memset(ones[:], 1.0)
        minus_half = sbuf.tile([P, 1], F32)
        nc.gpsimd.memset(minus_half[:], -0.5)
        table_warmer = sbuf.tile([P, 1], F32)
        nc.scalar.activation(out=table_warmer[:], in_=minus_half[:], func=ACT.Sin)
        partition_index = sbuf.tile([P, TILES], I32)
        nc.gpsimd.iota(partition_index[:], pattern=[[0, TILES]], base=0, channel_multiplier=1)
        tile_index = sbuf.tile([P, TILES], I32)
        nc.gpsimd.iota(tile_index[:], pattern=[[1, TILES]], base=0, channel_multiplier=0)
        source_minus_row = sbuf.tile([P, POSITIONS // TILES, BATCH], F32)
        nc.gpsimd.iota(
            source_minus_row[:],
            pattern=[[1, POSITIONS // TILES], [POSITIONS // TILES, BATCH]],
            base=0,
            channel_multiplier=-1,
            allow_small_or_imprecise_dtypes=True,
        )
        permutation = sbuf.tile([P, P], BF16)
        nc.gpsimd.tensor_scalar(
            out=permutation[:],
            in0=source_minus_row[:].rearrange("i lh b -> i (lh b)"),
            scalar1=0.0,
            scalar2=None,
            op0=ALU.is_equal,
        )

        theta = sbuf.tile([P, PAIRS], F32)
        nc.vector.memset(theta[:, 0:1], 1.0)
        for doubling in range(6):
            known = 1 << doubling
            nc.vector.tensor_scalar(
                out=theta[:, known : 2 * known],
                in0=theta[:, 0:known],
                scalar1=10000.0 ** (-known / 64.0),
                scalar2=None,
                op0=ALU.mult,
            )
        position_base = sbuf.tile([P, TILES], I32)
        nc.vector.tensor_scalar(
            out=position_base[:], in0=partition_index[:], scalar1=124, scalar2=None, op0=ALU.bitwise_and
        )
        position = sbuf.tile([P, TILES], I32)
        nc.vector.tensor_tensor(out=position[:], in0=position_base[:], in1=tile_index[:], op=ALU.bitwise_or)
        position_turns = sbuf.tile([P, TILES], F32)
        nc.vector.tensor_scalar(out=position_turns[:], in0=position[:], scalar1=TURN, scalar2=None, op0=ALU.mult)
        turns = sbuf.tile([P, TILES, PAIRS], F32)
        for j in range(TILES):
            nc.vector.tensor_scalar(
                out=turns[:, j, :],
                in0=theta[:],
                scalar1=position_turns[:, j : j + 1],
                scalar2=0.25,
                op0=ALU.mult,
                op1=ALU.add,
            )

        g_all = psum.tile([P, EMBED], BF16, tag="bank")
        for half in range(2):
            cols = slice(512 * half, 512 * half + 512)
            nc.tensor.matmul(out=g_all[:, cols], lhsT=ones[:], rhs=g_row[:, cols], start=True, stop=True)

        rstd = []
        for j in range(TILES):
            mean_eps = sbuf.tile([P, 1], F32, name="mean_eps%d" % j)
            mean_a = sbuf.tile([P, 1], F32, name="mean_a%d" % j)
            if j < HALVED_TILES:
                squares_a = sbuf.tile([P, EMBED // 2], BF16, name="squares_a%d" % j)
                nc.scalar.activation(
                    out=squares_a[:],
                    in_=x_tiles[j][:, 0 : EMBED // 2],
                    func=ACT.Square,
                    scale=1.0 / 32.0,
                    accum_out=mean_a[:],
                )
                squares_b = sbuf.tile([P, EMBED // 2], F32, name="squares_b%d" % j)
                mean_b = sbuf.tile([P, 1], F32, name="mean_b%d" % j)
                nc.vector.scalar_tensor_tensor(
                    out=squares_b[:],
                    in0=x_tiles[j][:, EMBED // 2 : EMBED],
                    scalar=1.0 / 1024.0,
                    in1=x_tiles[j][:, EMBED // 2 : EMBED],
                    op0=ALU.mult,
                    op1=ALU.mult,
                    accum_out=mean_b[:],
                )
                nc.gpsimd.tensor_scalar(
                    out=mean_eps[:], in0=mean_a[:], scalar1=mean_b[:, 0:1], scalar2=EPS, op0=ALU.add, op1=ALU.add
                )
            else:
                squares_a = sbuf.tile([P, EMBED], BF16, name="squares_a%d" % j)
                nc.scalar.activation(
                    out=squares_a[:], in_=x_tiles[j][:], func=ACT.Square, scale=1.0 / 32.0, accum_out=mean_a[:]
                )
                nc.gpsimd.tensor_scalar(
                    out=mean_eps[:], in0=mean_a[:], scalar1=1.0, scalar2=EPS, op0=ALU.mult, op1=ALU.add
                )
            rstd_j = sbuf.tile([P, 1], F32, name="rstd%d" % j)
            nc.gpsimd.tensor_tensor(out=rstd_j[:], in0=mean_eps[:], in1=minus_half[:], op=ALU.pow)
            rstd.append(rstd_j)

        whole_turns_int = sbuf.tile([P, TILES, PAIRS], I32)
        nc.vector.tensor_copy(out=whole_turns_int[:], in_=turns[:])
        whole_turns = sbuf.tile([P, TILES, PAIRS], F32)
        nc.vector.tensor_copy(out=whole_turns[:], in_=whole_turns_int[:])
        rest = sbuf.tile([P, TILES, PAIRS], F32)
        nc.vector.tensor_tensor(out=rest[:], in0=turns[:], in1=whole_turns[:], op=ALU.subtract)
        minus_rest = sbuf.tile([P, TILES, PAIRS], F32)
        nc.vector.scalar_tensor_tensor(
            out=minus_rest[:], in0=rest[:], scalar=0.5, in1=rest[:], op0=ALU.is_gt, op1=ALU.subtract
        )
        cosines = sbuf.tile([P, TILES, PAIRS, 2], F32)
        nc.scalar.activation(
            out=cosines[:],
            in_=minus_rest[:].unsqueeze(3).to_broadcast([P, TILES, PAIRS, 2]),
            func=ACT.Sin,
            scale=-2.0 * math.pi,
        )

        h_t = []
        for j in range(TILES):
            h_j = sbuf.tile([P, EMBED], BF16, name="h%d" % j)
            nc.vector.scalar_tensor_tensor(
                out=h_j[:], in0=x_tiles[j][:], scalar=rstd[j][:, 0:1], in1=g_all[:], op0=ALU.mult, op1=ALU.mult
            )
            h_t_j = psum.tile([P, PASSES * PACK, P], BF16, tag="bank", name="h_t%d" % j)
            for ut in range(PASSES * PACK):
                nc.tensor.transpose(out=h_t_j[:, ut, :], in_=h_j[:, P * ut : P * ut + P], identity=permutation[:])
            h_t.append(h_t_j)

        w_grouped = [
            sbuf.tile([P, PASSES, CHUNKS[c][2], PACK], BF16, name="w_grouped%d" % c, align_bytes=64)
            for c in range(n_chunks)
        ]

        def regroup(copy, c, u, n0, n1):
            copy(
                out=w_grouped[c][:, u, n0:n1, :].rearrange("p (run n) t -> p run t n", n=4),
                in_=w_rows[c][:, u, :, n0:n1].rearrange("p t (run n) -> p run t n", n=4),
            )

        def regroup_on_vector(c, u):
            regroup(nc.vector.tensor_copy, c, u, 0, VECTOR_COLS[(c, u)])

        def regroup_on_scalar(c, u):
            n0 = VECTOR_COLS.get((c, u), 0)
            n1 = CHUNKS[c][2] - GPSIMD_COLS.get((c, u), 0)
            if n0 < n1:
                regroup(nc.scalar.copy, c, u, n0, n1)

        def regroup_on_gpsimd(c, u, one):
            width = CHUNKS[c][2]
            for n0 in range(width - GPSIMD_COLS[(c, u)], width, 128):
                nc.gpsimd.tensor_scalar(
                    out=w_grouped[c][:, u, n0 : n0 + 128, :],
                    in0=w_rows[c][:, u, :, n0 : n0 + 128].rearrange("p t n -> p n t"),
                    scalar1=one,
                    scalar2=0.0,
                    op0=ALU.mult,
                    op1=ALU.add,
                )

        def one_written_by_vector_now(c):
            one = sbuf.tile([P, 1], F32, name="one%d" % c)
            nc.vector.memset(one[:], 1.0)
            return one[:, 0:1]

        regroup_on_gpsimd(0, 1, 1.0)

        regroup_on_scalar(0, 0)
        h_grouped = []
        for j in range(TILES):
            h_grouped_j = sbuf.tile([P, PASSES, P, PACK], BF16, name="h_grouped%d" % j, align_bytes=64)
            nc.scalar.copy(out=h_grouped_j[:], in_=h_t[j][:].rearrange("p (u t) col -> p u col t", t=PACK))
            h_grouped.append(h_grouped_j)
        for c in range(n_chunks):
            for u in range(PASSES):
                if (c, u) != (0, 0):
                    regroup_on_scalar(c, u)

        h_words = sbuf.tile([P, TILES, PASSES * P], U32, align_bytes=64)
        h_scales = sbuf.tile([P, TILES, PASSES * P], U8, align_bytes=64)
        w_words = [
            sbuf.tile([P, PASSES, CHUNKS[c][2]], U32, name="w_words%d" % c, align_bytes=64) for c in range(n_chunks)
        ]
        w_scales = [
            sbuf.tile([P, PASSES, CHUNKS[c][2]], U8, name="w_scales%d" % c, align_bytes=64) for c in range(n_chunks)
        ]
        sums = {}

        def quantise_h(j):
            nc.vector.quantize_mx(
                out=h_words[:, j, :].bitcast(FP8X4),
                scales=h_scales[:, j, :],
                in_=h_grouped[j][:].rearrange("p u col t -> p (u col t)"),
            )

        def quantise_w(c, u):
            nc.vector.quantize_mx(
                out=w_words[c][:, u, :].bitcast(FP8X4),
                scales=w_scales[c][:, u, :],
                in_=w_grouped[c][:, u, :, :].rearrange("p n t -> p (n t)"),
            )

        def multiply(c, u):
            if u == 0:
                sums[c] = [
                    psum.tile([P, CHUNKS[c][2]], F32, tag="bank", name="sums%d_%d" % (c, j)) for j in range(TILES)
                ]
            for j in range(TILES):
                nc.tensor.matmul_mx(
                    out=sums[c][j][:],
                    lhsT=h_words[:, j, P * u : P * u + P].bitcast(FP8X4),
                    lhsT_scale=h_scales[:, j, P * u : P * u + P],
                    rhs=w_words[c][:, u, :].bitcast(FP8X4),
                    rhs_scale=w_scales[c][:, u, :],
                    start=(u == 0),
                    stop=(u == PASSES - 1),
                )

        def quantise_and_multiply(c, u):
            quantise_w(c, u)
            multiply(c, u)

        def rope_and_store(c):
            which, first, width = CHUNKS[c]
            out = out_0 if which == 0 else out_1
            heads = width // HEAD_DIM
            head0 = first // HEAD_DIM
            result = sbuf.tile([P, heads, TILES, HEAD_DIM], F32, name="result%d" % c)
            for j in range(TILES):
                cosines_j = cosines[:, j, :, :].rearrange("p m twice -> p (m twice)")
                nc.vector.tensor_tensor(
                    out=result[:, :, j, :],
                    in0=sums[c][j][:].rearrange("p (head d) -> p head d", d=HEAD_DIM),
                    in1=cosines_j.unsqueeze(1).to_broadcast([P, heads, HEAD_DIM]),
                    op=ALU.mult,
                )
            for b in range(BATCH):
                nc.sync.dma_start(
                    out=out[b, head0 : head0 + heads, :, :].rearrange("head (lh j) d -> lh head (j d)", j=TILES),
                    in_=result[b:P:BATCH, :, :, :].rearrange("p head j d -> p head (j d)"),
                )

        quantise_h(0)
        regroup_on_vector(0, 0)
        quantise_h(1)
        quantise_w(0, 0)
        quantise_h(2)
        regroup_on_vector(0, 1)
        quantise_h(3)
        regroup_on_vector(1, 0)
        multiply(0, 0)
        for c in range(n_chunks - 2):
            quantise_and_multiply(c, 1)
            quantise_and_multiply(c + 1, 0)
            regroup_on_gpsimd(c + 2, 0, one_written_by_vector_now(c))
            rope_and_store(c)
        quantise_and_multiply(n_chunks - 2, 1)
        quantise_and_multiply(n_chunks - 1, 0)
        quantise_and_multiply(n_chunks - 1, 1)
        rope_and_store(n_chunks - 2)
        rope_and_store(n_chunks - 1)
